import numpy as np
import ml_dtypes


def mxq(x, axis, fmt="e4m3"):
    dtype, down = {"e4m3": (ml_dtypes.float8_e4m3fn, 7), "e5m2": (ml_dtypes.float8_e5m2, 14)}[fmt]
    v = np.moveaxis(np.asarray(x, np.float32).astype(ml_dtypes.bfloat16).astype(np.float64), axis, -1)
    blocks = v.reshape(v.shape[:-1] + (-1, 32))
    amax = np.abs(blocks).max(-1, keepdims=True)
    byte = np.maximum(np.where(amax > 0, np.frexp(amax)[1] - 1 + 127, 0) - down, 1)
    scale = np.exp2(byte - 127.0)
    codes = (blocks / scale).astype(np.float32).astype(dtype).astype(np.float64)
    return np.moveaxis((codes * scale).reshape(v.shape), -1, axis)


WIDE = False


def mx_kscale(k):
    if not WIDE:
        return np.ones(k)
    levels = np.array([10, -10, 5, -5, 0])
    a = np.random.permutation(np.resize(levels, k // 512 * 4)).reshape(k // 512, 4)
    idx = np.arange(k)
    return np.exp2(a[idx // 512, idx % 128 // 32])


BF16 = ml_dtypes.bfloat16


def bf(x):
    return np.asarray(x, np.float32).astype(BF16)


def f64(x):
    return np.asarray(x).astype(np.float64)


E2M1 = np.array([0.0, 0.5, 1.0, 1.5, 2.0, 3.0, 4.0, 6.0, -0.0, -0.5, -1.0, -1.5, -2.0, -3.0, -4.0, -6.0])


def pack_weight(w, fmt):
    k, n = w.shape
    w = f64(bf(w)).reshape(k // 32, 32, n)
    amax = np.abs(w).max(1)
    if fmt == "e4m3":
        byte = np.frexp(amax)[1] - 1 + 127 - 7
    else:
        mant, ex = np.frexp(amax / 6.0)
        byte = np.where(mant > 0.5, ex, ex - 1) + 127
    byte = np.clip(np.where(amax > 0, byte, 1), 1, 254)
    scaled = (w * np.exp2(127.0 - byte)[:, None, :]).reshape(k, n).astype(np.float32)
    by_word = np.ascontiguousarray(scaled.reshape(k // 512, 128, 4, n).transpose(0, 1, 3, 2))
    if fmt == "e4m3":
        words = by_word.astype(ml_dtypes.float8_e4m3fn).view(np.uint8)
    else:
        c = by_word.astype(ml_dtypes.float4_e2m1fn).view(np.uint8) & 0xF
        words = c[..., 0::2] | (c[..., 1::2] << 4)
    return np.ascontiguousarray(words), np.ascontiguousarray(byte.astype(np.uint8).reshape(k // 512, 16, n))


def unpack_weight(words, scales, fmt):
    g, p, n, _ = words.shape
    if fmt == "e4m3":
        vals = np.ascontiguousarray(words).view(ml_dtypes.float8_e4m3fn).astype(np.float64)
    else:
        nib = np.empty((g, p, n, 4), np.uint8)
        nib[..., 0::2] = words & 0xF
        nib[..., 1::2] = words >> 4
        vals = E2M1[nib]
    vals = vals * np.repeat(np.exp2(scales.astype(np.float64) - 127.0), 8, axis=1)[..., None]
    return vals.transpose(0, 1, 3, 2).reshape(g * 512, n)


B, S, I0, I1, I2, O0, O1, O2 = 2, 256, 1024, 2048, 4096, 1024, 1024, 2048
FMT = "e4m3"


def init_w(out_d, in_d, s):
    w = np.random.uniform(-1.0, 1.0, (out_d, in_d)) / np.sqrt(in_d) / s[None, :in_d]
    return pack_weight(np.ascontiguousarray(w.T), FMT)


def setup_inputs():
    s = mx_kscale(I2)
    x = bf(np.random.standard_normal((B, S, I2)) * s)
    w0_words, w0_scales = init_w(O0, I0, s)
    w1_words, w1_scales = init_w(O1, I1, s)
    w2_words, w2_scales = init_w(O2, I2, s)
    return {"x": x, "W0_words": w0_words, "W0_scales": w0_scales, "W1_words": w1_words, "W1_scales": w1_scales, "W2_words": w2_words, "W2_scales": w2_scales}


def reference(x, W0_words, W0_scales, W1_words, W1_scales, W2_words, W2_scales):
    xq = mxq(f64(x), 2, "e4m3")
    y0 = xq[..., :I0] @ unpack_weight(W0_words, W0_scales, FMT)
    y1 = xq[..., :I1] @ unpack_weight(W1_words, W1_scales, FMT)
    y2 = xq[..., :I2] @ unpack_weight(W2_words, W2_scales, FMT)
    return np.concatenate([y0, y1, y2], axis=-1)

@@ -1,0 +1,174 @@
+from contextlib import ExitStack
+
+import concourse.mybir as mybir
+from concourse.masks import make_identity
+
+F32 = mybir.dt.float32
+BF16 = mybir.dt.bfloat16
+I32 = mybir.dt.int32
+U32 = mybir.dt.uint32
+U8 = mybir.dt.uint8
+FP8X4 = mybir.dt.float8_e4m3fn_x4
+
+P = 128
+K_PASS = 512
+TOKENS = 512
+TOKEN_TILES = TOKENS // P
+FEATURES_IN = 4096
+X_BLOCK = 1024
+PASSES_PER_BLOCK = X_BLOCK // K_PASS
+X_BLOCKS = FEATURES_IN // X_BLOCK
+N_CHUNK = 512
+PLANES_PER_TILE = 4
+SCALE_ROWS = 4
+QUADRANTS = 4
+
+FLOPS = 2 * TOKENS * (1024 * 1024 + 2048 * 1024 + 4096 * 2048)
+
+
+def tile_naivematryoshkalinear_kernel(
+    tc, x, W0_words, W0_scales, W1_words, W1_scales, W2_words, W2_scales, out
+):
+    nc = tc.nc
+    x_rows = x.flatten_outer_dims()
+    out_rows = out.flatten_outer_dims()
+
+    weights = [
+        dict(words=W0_words, scales=W0_scales, first_column=0),
+        dict(words=W1_words, scales=W1_scales, first_column=1024),
+        dict(words=W2_words, scales=W2_scales, first_column=2048),
+    ]
+    for w in weights:
+        w["passes"] = w["words"].shape[0]
+        w["columns"] = w["words"].shape[2]
+        w["chunks"] = {}
+        w["planes"] = []
+
+    with ExitStack() as ctx:
+        ctx.enter_context(tc.manual_schedule())
+        keep = ctx.enter_context(tc.tile_pool(name="keep", bufs=1))
+        x_pool = ctx.enter_context(tc.tile_pool(name="x_pool", bufs=X_BLOCKS * TOKEN_TILES))
+        stage = ctx.enter_context(tc.tile_pool(name="stage", bufs=4))
+        results = ctx.enter_context(tc.tile_pool(name="results", bufs=32))
+        psum_x = ctx.enter_context(tc.psum_pool(name="psum_x", bufs=4))
+        psum_acc = ctx.enter_context(tc.psum_pool(name="psum_acc", bufs=4))
+
+        identity = keep.tile([P, P], F32)
+        make_identity(nc, identity[:])
+
+        for i, w in enumerate(weights):
+            for first_pass in range(0, w["passes"], PLANES_PER_TILE):
+                planes = keep.tile(
+                    [P, w["columns"]], U8, name="w%d_planes%d" % (i, first_pass), align_bytes=64
+                )
+                nc.vector.memset(planes[:].bitcast(I32), 0)
+                w["planes"].append(planes)
+
+        x_codes = keep.tile([P, X_BLOCKS, TOKEN_TILES, PASSES_PER_BLOCK * P], U32, align_bytes=64)
+        x_scales = keep.tile([P, X_BLOCKS, TOKEN_TILES, PASSES_PER_BLOCK * P], U8, align_bytes=64)
+
+        x_raw = {}
+
+        def load_x_block(b):
+            for m in range(TOKEN_TILES):
+                raw = x_pool.tile([P, X_BLOCK], BF16, name="x_raw")
+                nc.sync.dma_start(
+                    out=raw[:],
+                    in_=x_rows[m * P : (m + 1) * P, b * X_BLOCK : (b + 1) * X_BLOCK],
+                )
+                x_raw[(b, m)] = raw
+
+        def load_scales(w):
+            for s, planes in enumerate(w["planes"]):
+                first_pass = s * PLANES_PER_TILE
+                n_passes = min(PLANES_PER_TILE, w["passes"] - first_pass)
+                for q in range(QUADRANTS):
+                    nc.sync.dma_start(
+                        out=planes[32 * q : 32 * q + SCALE_ROWS * n_passes, :].bitcast(I32),
+                        in_=w["scales"][
+                            first_pass : first_pass + n_passes, SCALE_ROWS * q : SCALE_ROWS * (q + 1), :
+                        ].bitcast(I32),
+                    )
+
+        def load_words(i, c):
+            w = weights[i]
+            words = keep.tile([P, w["passes"], N_CHUNK], I32, name="w%d_words%d" % (i, c), align_bytes=64)
+            by_partition = w["words"].rearrange("g p n t -> p g (n t)")
+            nc.sync.dma_start(
+                out=words[:],
+                in_=by_partition[:, :, 4 * N_CHUNK * c : 4 * N_CHUNK * (c + 1)].bitcast(I32),
+            )
+            w["chunks"][c] = words
+
+        load_x_block(0)
+        load_scales(weights[0])
+        load_scales(weights[1])
+        load_words(0, 0)
+        load_words(0, 1)
+        load_x_block(1)
+        load_words(1, 0)
+        load_words(1, 1)
+        load_scales(weights[2])
+        load_x_block(2)
+        load_x_block(3)
+        for c in range(4):
+            load_words(2, c)
+
+        def quantise_x_block(b):
+            for m in range(TOKEN_TILES):
+                words = x_raw[(b, m)][:].bitcast(F32)
+                flipped = psum_x.tile([P, PASSES_PER_BLOCK, 2, P], F32)
+                for g in range(PASSES_PER_BLOCK):
+                    for u in range(2):
+                        nc.tensor.transpose(
+                            flipped[:, g, u, :],
+                            words[:, 256 * g + u : 256 * (g + 1) : 2],
+                            identity[:],
+                        )
+                grouped = stage.tile([P, PASSES_PER_BLOCK * P * 4], BF16, align_bytes=64)
+                nc.scalar.copy(
+                    out=grouped[:].bitcast(F32).rearrange("p (g r u) -> p g r u", g=PASSES_PER_BLOCK, u=2),
+                    in_=flipped[:].rearrange("p g u r -> p g r u"),
+                )
+                nc.vector.quantize_mx(
+                    out=x_codes[:, b, m, :].bitcast(FP8X4),
+                    scales=x_scales[:, b, m, :],
+                    in_=grouped[:],
+                )
+
+        def multiply_chunk(i, c):
+            w = weights[i]
+            words = w["chunks"][c]
+            for m in range(TOKEN_TILES):
+                acc = psum_acc.tile([P, N_CHUNK], F32)
+                for g in range(w["passes"]):
+                    b, g_in_block = divmod(g, PASSES_PER_BLOCK)
+                    tokens = slice(g_in_block * P, (g_in_block + 1) * P)
+                    s, j = divmod(g, PLANES_PER_TILE)
+                    nc.tensor.matmul_mx(
+                        out=acc[:],
+                        lhsT=x_codes[:, b, m, tokens].bitcast(FP8X4),
+                        lhsT_scale=x_scales[:, b, m, tokens],
+                        rhs=words[:, g, :].bitcast(FP8X4),
+                        rhs_scale=w["planes"][s][SCALE_ROWS * j : P, c * N_CHUNK : (c + 1) * N_CHUNK],
+                        start=(g == 0),
+                        stop=(g == w["passes"] - 1),
+                    )
+                result = results.tile([P, N_CHUNK], F32)
+                if m % 2 == 0:
+                    nc.vector.tensor_copy(out=result[:], in_=acc[:])
+                else:
+                    nc.scalar.copy(out=result[:], in_=acc[:])
+                first = w["first_column"] + c * N_CHUNK
+                nc.sync.dma_start(out=out_rows[m * P : (m + 1) * P, first : first + N_CHUNK], in_=result[:])
+
+        quantise_x_block(0)
+        multiply_chunk(0, 0)
+        quantise_x_block(1)
+        multiply_chunk(0, 1)
+        multiply_chunk(1, 0)
+        quantise_x_block(2)
+        quantise_x_block(3)
+        multiply_chunk(1, 1)
+        for c in range(4):
+            multiply_chunk(2, c)

@@ -78,41 +78,53 @@ def tile_naivematryoshkalinear_kernel(
                 )
                 x_raw[(b, m)] = raw
 
-        def load_scales(w):
-            for s, planes in enumerate(w["planes"]):
-                first_pass = s * PLANES_PER_TILE
-                n_passes = min(PLANES_PER_TILE, w["passes"] - first_pass)
-                for q in range(QUADRANTS):
-                    nc.sync.dma_start(
-                        out=planes[32 * q : 32 * q + SCALE_ROWS * n_passes, :].bitcast(I32),
-                        in_=w["scales"][
-                            first_pass : first_pass + n_passes, SCALE_ROWS * q : SCALE_ROWS * (q + 1), :
-                        ].bitcast(I32),
-                    )
+        def load_scales(w, s):
+            planes = w["planes"][s]
+            first_pass = s * PLANES_PER_TILE
+            n_passes = min(PLANES_PER_TILE, w["passes"] - first_pass)
+            for q in range(QUADRANTS):
+                nc.sync.dma_start(
+                    out=planes[32 * q : 32 * q + SCALE_ROWS * n_passes, :].bitcast(I32),
+                    in_=w["scales"][
+                        first_pass : first_pass + n_passes, SCALE_ROWS * q : SCALE_ROWS * (q + 1), :
+                    ].bitcast(I32),
+                )
 
-        def load_words(i, c):
+        def load_words(i, c, first_pass, n_passes):
             w = weights[i]
-            words = keep.tile([P, w["passes"], N_CHUNK], I32, name="w%d_words%d" % (i, c), align_bytes=64)
+            if c not in w["chunks"]:
+                w["chunks"][c] = keep.tile(
+                    [P, w["passes"], N_CHUNK], I32, name="w%d_words%d" % (i, c), align_bytes=64
+                )
             by_partition = w["words"].rearrange("g p n t -> p g (n t)")
             nc.sync.dma_start(
-                out=words[:],
-                in_=by_partition[:, :, 4 * N_CHUNK * c : 4 * N_CHUNK * (c + 1)].bitcast(I32),
+                out=w["chunks"][c][:, first_pass : first_pass + n_passes, :],
+                in_=by_partition[
+                    :, first_pass : first_pass + n_passes, 4 * N_CHUNK * c : 4 * N_CHUNK * (c + 1)
+                ].bitcast(I32),
             )
-            w["chunks"][c] = words
 
         load_x_block(0)
-        load_scales(weights[0])
-        load_scales(weights[1])
-        load_words(0, 0)
-        load_words(0, 1)
+        load_scales(weights[0], 0)
+        load_words(0, 0, 0, 1)
+        load_words(0, 0, 1, 1)
+        load_words(0, 1, 0, 2)
         load_x_block(1)
-        load_words(1, 0)
-        load_words(1, 1)
-        load_scales(weights[2])
+        load_scales(weights[1], 0)
+        load_words(1, 0, 0, 2)
+        load_words(1, 0, 2, 2)
+        load_words(1, 1, 0, 4)
+        load_scales(weights[2], 0)
+        load_words(2, 0, 0, 2)
         load_x_block(2)
+        load_words(2, 0, 2, 2)
         load_x_block(3)
-        for c in range(4):
-            load_words(2, c)
+        load_scales(weights[2], 1)
+        load_words(2, 0, 4, 4)
+        load_words(2, 1, 0, 4)
+        load_words(2, 1, 4, 4)
+        load_words(2, 2, 0, 8)
+        load_words(2, 3, 0, 8)
 
         def quantise_x_block(b):
             for m in range(TOKEN_TILES):
@@ -136,25 +148,28 @@ def tile_naivematryoshkalinear_kernel(
                     in_=grouped[:],
                 )
 
-        def multiply_chunk(i, c):
+        open_banks = {}
+
+        def one_pass(i, c, m, g):
             w = weights[i]
-            words = w["chunks"][c]
-            for m in range(TOKEN_TILES):
-                acc = psum_acc.tile([P, N_CHUNK], F32)
-                for g in range(w["passes"]):
-                    b, g_in_block = divmod(g, PASSES_PER_BLOCK)
-                    tokens = slice(g_in_block * P, (g_in_block + 1) * P)
-                    s, j = divmod(g, PLANES_PER_TILE)
-                    nc.tensor.matmul_mx(
-                        out=acc[:],
-                        lhsT=x_codes[:, b, m, tokens].bitcast(FP8X4),
-                        lhsT_scale=x_scales[:, b, m, tokens],
-                        rhs=words[:, g, :].bitcast(FP8X4),
-                        rhs_scale=w["planes"][s][SCALE_ROWS * j : P, c * N_CHUNK : (c + 1) * N_CHUNK],
-                        start=(g == 0),
-                        stop=(g == w["passes"] - 1),
-                    )
-                result = results.tile([P, N_CHUNK], F32)
+            if g == 0:
+                acc = psum_acc.tile([P, N_CHUNK], F32, name="acc")
+                open_banks[(i, c, m)] = acc
+            acc = open_banks[(i, c, m)]
+            b, g_in_block = divmod(g, PASSES_PER_BLOCK)
+            tokens = slice(g_in_block * P, (g_in_block + 1) * P)
+            s, j = divmod(g, PLANES_PER_TILE)
+            nc.tensor.matmul_mx(
+                out=acc[:],
+                lhsT=x_codes[:, b, m, tokens].bitcast(FP8X4),
+                lhsT_scale=x_scales[:, b, m, tokens],
+                rhs=w["chunks"][c][:, g, :].bitcast(FP8X4),
+                rhs_scale=w["planes"][s][SCALE_ROWS * j : P, c * N_CHUNK : (c + 1) * N_CHUNK],
+                start=(g == 0),
+                stop=(g == w["passes"] - 1),
+            )
+            if g == w["passes"] - 1:
+                result = results.tile([P, N_CHUNK], F32, name="result")
                 if m % 2 == 0:
                     nc.vector.tensor_copy(out=result[:], in_=acc[:])
                 else:
@@ -162,13 +177,27 @@ def tile_naivematryoshkalinear_kernel(
                 first = w["first_column"] + c * N_CHUNK
                 nc.sync.dma_start(out=out_rows[m * P : (m + 1) * P, first : first + N_CHUNK], in_=result[:])
 
+        def passes_first(i, c, first_pass, n_passes):
+            for g in range(first_pass, first_pass + n_passes):
+                for m in range(TOKEN_TILES):
+                    one_pass(i, c, m, g)
+
+        def tiles_first(i, c):
+            for m in range(TOKEN_TILES):
+                for g in range(weights[i]["passes"]):
+                    one_pass(i, c, m, g)
+
         quantise_x_block(0)
-        multiply_chunk(0, 0)
+        passes_first(0, 0, 0, 2)
+        passes_first(0, 1, 0, 2)
         quantise_x_block(1)
-        multiply_chunk(0, 1)
-        multiply_chunk(1, 0)
+        passes_first(1, 0, 0, 4)
+        passes_first(1, 1, 0, 4)
+        passes_first(2, 0, 0, 2)
         quantise_x_block(2)
+        passes_first(2, 0, 2, 2)
         quantise_x_block(3)
-        multiply_chunk(1, 1)
-        for c in range(4):
-            multiply_chunk(2, c)
+        passes_first(2, 0, 4, 4)
+        passes_first(2, 1, 0, 8)
+        passes_first(2, 2, 0, 8)
+        tiles_first(2, 3)

@@ -47,7 +47,8 @@ def tile_naivematryoshkalinear_kernel(
     with ExitStack() as ctx:
         ctx.enter_context(tc.manual_schedule())
         keep = ctx.enter_context(tc.tile_pool(name="keep", bufs=1))
-        x_pool = ctx.enter_context(tc.tile_pool(name="x_pool", bufs=X_BLOCKS * TOKEN_TILES))
+        x_pool = ctx.enter_context(tc.tile_pool(name="x_pool", bufs=(X_BLOCKS - 1) * TOKEN_TILES))
+        sorted_pool = ctx.enter_context(tc.tile_pool(name="sorted_pool", bufs=2 * TOKEN_TILES))
         stage = ctx.enter_context(tc.tile_pool(name="stage", bufs=4))
         results = ctx.enter_context(tc.tile_pool(name="results", bufs=32))
         psum_x = ctx.enter_context(tc.psum_pool(name="psum_x", bufs=4))
@@ -104,27 +105,17 @@ def tile_naivematryoshkalinear_kernel(
                 ].bitcast(I32),
             )
 
-        load_x_block(0)
-        load_scales(weights[0], 0)
-        load_words(0, 0, 0, 1)
-        load_words(0, 0, 1, 1)
-        load_words(0, 1, 0, 2)
-        load_x_block(1)
-        load_scales(weights[1], 0)
-        load_words(1, 0, 0, 2)
-        load_words(1, 0, 2, 2)
-        load_words(1, 1, 0, 4)
-        load_scales(weights[2], 0)
-        load_words(2, 0, 0, 2)
-        load_x_block(2)
-        load_words(2, 0, 2, 2)
-        load_x_block(3)
-        load_scales(weights[2], 1)
-        load_words(2, 0, 4, 4)
-        load_words(2, 1, 0, 4)
-        load_words(2, 1, 4, 4)
-        load_words(2, 2, 0, 8)
-        load_words(2, 3, 0, 8)
+
+        x_sorted = {}
+
+        def sort_x_block(b):
+            for m in range(TOKEN_TILES):
+                by_parity = sorted_pool.tile([P, X_BLOCK // 2], F32, name="by_parity")
+                nc.vector.tensor_copy(
+                    out=by_parity[:].rearrange("p (g u w) -> p g u w", g=PASSES_PER_BLOCK, u=2),
+                    in_=x_raw[(b, m)][:].bitcast(F32).rearrange("p (g w u) -> p g u w", g=PASSES_PER_BLOCK, u=2),
+                )
+                x_sorted[(b, m)] = by_parity
 
         def quantise_x_block(b):
             for m in range(TOKEN_TILES):
@@ -132,11 +123,11 @@ def tile_naivematryoshkalinear_kernel(
                 flipped = psum_x.tile([P, PASSES_PER_BLOCK, 2, P], F32)
                 for g in range(PASSES_PER_BLOCK):
                     for u in range(2):
-                        nc.tensor.transpose(
-                            flipped[:, g, u, :],
-                            words[:, 256 * g + u : 256 * (g + 1) : 2],
-                            identity[:],
-                        )
+                        if (b, m) in x_sorted:
+                            columns = x_sorted[(b, m)][:, (2 * g + u) * P : (2 * g + u + 1) * P]
+                        else:
+                            columns = words[:, 256 * g + u : 256 * (g + 1) : 2]
+                        nc.tensor.transpose(flipped[:, g, u, :], columns, identity[:])
                 grouped = stage.tile([P, PASSES_PER_BLOCK * P * 4], BF16, align_bytes=64)
                 nc.scalar.copy(
                     out=grouped[:].bitcast(F32).rearrange("p (g r u) -> p g r u", g=PASSES_PER_BLOCK, u=2),
@@ -187,13 +178,39 @@ def tile_naivematryoshkalinear_kernel(
                 for g in range(weights[i]["passes"]):
                     one_pass(i, c, m, g)
 
+        load_x_block(0)
+        load_scales(weights[0], 0)
+        load_words(0, 0, 0, 1)
+        load_words(0, 0, 1, 1)
+        load_words(0, 1, 0, 2)
+        load_x_block(1)
+        load_scales(weights[1], 0)
+        load_words(1, 0, 0, 2)
+        load_words(1, 0, 2, 2)
+        load_words(1, 1, 0, 4)
+        load_scales(weights[2], 0)
+        load_words(2, 0, 0, 2)
+        load_x_block(2)
+        load_words(2, 0, 2, 2)
         quantise_x_block(0)
+        load_x_block(3)
+        load_scales(weights[2], 1)
+        load_words(2, 0, 4, 4)
+        load_words(2, 1, 0, 4)
+        load_words(2, 1, 4, 4)
+        load_words(2, 2, 0, 8)
+        load_words(2, 3, 0, 8)
+
         passes_first(0, 0, 0, 2)
-        passes_first(0, 1, 0, 2)
+        passes_first(0, 1, 0, 1)
+        sort_x_block(1)
+        passes_first(0, 1, 1, 1)
         quantise_x_block(1)
         passes_first(1, 0, 0, 4)
         passes_first(1, 1, 0, 4)
+        sort_x_block(2)
         passes_first(2, 0, 0, 2)
+        sort_x_block(3)
         quantise_x_block(2)
         passes_first(2, 0, 2, 2)
         quantise_x_block(3)

@@ -168,14 +168,9 @@ def tile_naivematryoshkalinear_kernel(
                 first = w["first_column"] + c * N_CHUNK
                 nc.sync.dma_start(out=out_rows[m * P : (m + 1) * P, first : first + N_CHUNK], in_=result[:])
 
-        def passes_first(i, c, first_pass, n_passes):
-            for g in range(first_pass, first_pass + n_passes):
-                for m in range(TOKEN_TILES):
-                    one_pass(i, c, m, g)
-
-        def tiles_first(i, c):
+        def multiply(i, c, first_pass, n_passes):
             for m in range(TOKEN_TILES):
-                for g in range(weights[i]["passes"]):
+                for g in range(first_pass, first_pass + n_passes):
                     one_pass(i, c, m, g)
 
         load_x_block(0)
@@ -195,26 +190,30 @@ def tile_naivematryoshkalinear_kernel(
         quantise_x_block(0)
         load_x_block(3)
         load_scales(weights[2], 1)
-        load_words(2, 0, 4, 4)
+        load_words(2, 0, 4, 2)
+        load_words(2, 0, 6, 2)
         load_words(2, 1, 0, 4)
         load_words(2, 1, 4, 4)
         load_words(2, 2, 0, 8)
         load_words(2, 3, 0, 8)
 
-        passes_first(0, 0, 0, 2)
-        passes_first(0, 1, 0, 1)
+        multiply(0, 0, 0, 1)
+        multiply(0, 0, 1, 1)
         sort_x_block(1)
-        passes_first(0, 1, 1, 1)
+        multiply(0, 1, 0, 2)
         quantise_x_block(1)
-        passes_first(1, 0, 0, 4)
-        passes_first(1, 1, 0, 4)
+        multiply(1, 0, 0, 2)
+        multiply(1, 0, 2, 2)
+        multiply(1, 1, 0, 4)
         sort_x_block(2)
-        passes_first(2, 0, 0, 2)
+        multiply(2, 0, 0, 2)
         sort_x_block(3)
         quantise_x_block(2)
-        passes_first(2, 0, 2, 2)
+        multiply(2, 0, 2, 2)
         quantise_x_block(3)
-        passes_first(2, 0, 4, 4)
-        passes_first(2, 1, 0, 8)
-        passes_first(2, 2, 0, 8)
-        tiles_first(2, 3)
+        multiply(2, 0, 4, 2)
+        multiply(2, 0, 6, 2)
+        multiply(2, 1, 0, 4)
+        multiply(2, 1, 4, 4)
+        multiply(2, 2, 0, 8)
+        multiply(2, 3, 0, 8)

@@ -141,10 +141,10 @@ def tile_naivematryoshkalinear_kernel(
 
         open_banks = {}
 
-        def one_pass(i, c, m, g):
+        def one_pass(i, c, m, g, first=0, width=N_CHUNK):
             w = weights[i]
             if g == 0:
-                acc = psum_acc.tile([P, N_CHUNK], F32, name="acc")
+                acc = psum_acc.tile([P, width], F32, name="acc")
                 open_banks[(i, c, m)] = acc
             acc = open_banks[(i, c, m)]
             b, g_in_block = divmod(g, PASSES_PER_BLOCK)
@@ -154,22 +154,22 @@ def tile_naivematryoshkalinear_kernel(
                 out=acc[:],
                 lhsT=x_codes[:, b, m, tokens].bitcast(FP8X4),
                 lhsT_scale=x_scales[:, b, m, tokens],
-                rhs=w["chunks"][c][:, g, :].bitcast(FP8X4),
-                rhs_scale=w["planes"][s][SCALE_ROWS * j : P, c * N_CHUNK : (c + 1) * N_CHUNK],
+                rhs=w["chunks"][c][:, g, first : first + width].bitcast(FP8X4),
+                rhs_scale=w["planes"][s][SCALE_ROWS * j : P, c * N_CHUNK + first : c * N_CHUNK + first + width],
                 start=(g == 0),
                 stop=(g == w["passes"] - 1),
             )
             if g == w["passes"] - 1:
-                result = results.tile([P, N_CHUNK], F32, name="result")
-                if m % 2 == 0:
+                result = results.tile([P, width], F32, name="result")
+                if (m + first // width) % 2 == 0:
                     nc.vector.tensor_copy(out=result[:], in_=acc[:])
                 else:
                     nc.scalar.copy(out=result[:], in_=acc[:])
-                first = w["first_column"] + c * N_CHUNK
-                nc.sync.dma_start(out=out_rows[m * P : (m + 1) * P, first : first + N_CHUNK], in_=result[:])
+                column = w["first_column"] + c * N_CHUNK + first
+                nc.sync.dma_start(out=out_rows[m * P : (m + 1) * P, column : column + width], in_=result[:])
 
-        def multiply(i, c, first_pass, n_passes):
-            for m in range(TOKEN_TILES):
+        def multiply(i, c, first_pass, n_passes, token_tiles=TOKEN_TILES):
+            for m in range(token_tiles):
                 for g in range(first_pass, first_pass + n_passes):
                     one_pass(i, c, m, g)
 
@@ -216,4 +216,7 @@ def tile_naivematryoshkalinear_kernel(
         multiply(2, 1, 0, 4)
         multiply(2, 1, 4, 4)
         multiply(2, 2, 0, 8)
-        multiply(2, 3, 0, 8)
+        multiply(2, 3, 0, 8, token_tiles=TOKEN_TILES - 1)
+        for half in range(2):
+            for g in range(weights[2]["passes"]):
+                one_pass(2, 3, TOKEN_TILES - 1, g, first=half * (N_CHUNK // 2), width=N_CHUNK // 2)

@@ -119,14 +119,10 @@ def tile_naivematryoshkalinear_kernel(
 
         def quantise_x_block(b):
             for m in range(TOKEN_TILES):
-                words = x_raw[(b, m)][:].bitcast(F32)
                 flipped = psum_x.tile([P, PASSES_PER_BLOCK, 2, P], F32)
                 for g in range(PASSES_PER_BLOCK):
                     for u in range(2):
-                        if (b, m) in x_sorted:
-                            columns = x_sorted[(b, m)][:, (2 * g + u) * P : (2 * g + u + 1) * P]
-                        else:
-                            columns = words[:, 256 * g + u : 256 * (g + 1) : 2]
+                        columns = x_sorted[(b, m)][:, (2 * g + u) * P : (2 * g + u + 1) * P]
                         nc.tensor.transpose(flipped[:, g, u, :], columns, identity[:])
                 grouped = stage.tile([P, PASSES_PER_BLOCK * P * 4], BF16, align_bytes=64)
                 nc.scalar.copy(
@@ -168,8 +164,8 @@ def tile_naivematryoshkalinear_kernel(
                 column = w["first_column"] + c * N_CHUNK + first
                 nc.sync.dma_start(out=out_rows[m * P : (m + 1) * P, column : column + width], in_=result[:])
 
-        def multiply(i, c, first_pass, n_passes, token_tiles=TOKEN_TILES):
-            for m in range(token_tiles):
+        def multiply(i, c, first_pass, n_passes, first_tile=0, n_tiles=TOKEN_TILES):
+            for m in range(first_tile, first_tile + n_tiles):
                 for g in range(first_pass, first_pass + n_passes):
                     one_pass(i, c, m, g)
 
@@ -187,6 +183,7 @@ def tile_naivematryoshkalinear_kernel(
         load_words(2, 0, 0, 2)
         load_x_block(2)
         load_words(2, 0, 2, 2)
+        sort_x_block(0)
         quantise_x_block(0)
         load_x_block(3)
         load_scales(weights[2], 1)
@@ -197,8 +194,9 @@ def tile_naivematryoshkalinear_kernel(
         load_words(2, 2, 0, 8)
         load_words(2, 3, 0, 8)
 
-        multiply(0, 0, 0, 1)
-        multiply(0, 0, 1, 1)
+        multiply(0, 0, 0, 1, n_tiles=2)
+        multiply(0, 0, 1, 1, n_tiles=2)
+        multiply(0, 0, 0, 2, first_tile=2, n_tiles=2)
         sort_x_block(1)
         multiply(0, 1, 0, 2)
         quantise_x_block(1)
@@ -216,7 +214,7 @@ def tile_naivematryoshkalinear_kernel(
         multiply(2, 1, 0, 4)
         multiply(2, 1, 4, 4)
         multiply(2, 2, 0, 8)
-        multiply(2, 3, 0, 8, token_tiles=TOKEN_TILES - 1)
+        multiply(2, 3, 0, 8, n_tiles=TOKEN_TILES - 1)
         for half in range(2):
             for g in range(weights[2]["passes"]):
                 one_pass(2, 3, TOKEN_TILES - 1, g, first=half * (N_CHUNK // 2), width=N_CHUNK // 2)

@@ -57,6 +57,16 @@ def tile_naivematryoshkalinear_kernel(
         identity = keep.tile([P, P], F32)
         make_identity(nc, identity[:])
 
+        idle_operand = keep.tile([P, N_CHUNK], BF16, name="idle_operand")
+        nc.vector.memset(idle_operand[:], 0.0)
+        idle_bank = psum_acc.tile([P, N_CHUNK], F32, name="acc")
+
+        def idle_matmuls(count):
+            for r in range(count):
+                nc.tensor.matmul(
+                    out=idle_bank[:], lhsT=idle_operand[:, :P], rhs=idle_operand[:], start=True, stop=True
+                )
+
         for i, w in enumerate(weights):
             for first_pass in range(0, w["passes"], PLANES_PER_TILE):
                 planes = keep.tile(
@@ -124,6 +134,8 @@ def tile_naivematryoshkalinear_kernel(
                     for u in range(2):
                         columns = x_sorted[(b, m)][:, (2 * g + u) * P : (2 * g + u + 1) * P]
                         nc.tensor.transpose(flipped[:, g, u, :], columns, identity[:])
+                if b == 0:
+                    idle_matmuls(1)
                 grouped = stage.tile([P, PASSES_PER_BLOCK * P * 4], BF16, align_bytes=64)
                 nc.scalar.copy(
                     out=grouped[:].bitcast(F32).rearrange("p (g r u) -> p g r u", g=PASSES_PER_BLOCK, u=2),
@@ -183,6 +195,7 @@ def tile_naivematryoshkalinear_kernel(
         load_words(2, 0, 0, 2)
         load_x_block(2)
         load_words(2, 0, 2, 2)
+        idle_matmuls(4)
         sort_x_block(0)
         quantise_x_block(0)
         load_x_block(3)

@@ -41,6 +41,7 @@ def tile_naivematryoshkalinear_kernel(
     for w in weights:
         w["passes"] = w["words"].shape[0]
         w["columns"] = w["words"].shape[2]
+        w["tiles"] = {}
         w["chunks"] = {}
         w["planes"] = []
 
@@ -101,17 +102,20 @@ def tile_naivematryoshkalinear_kernel(
                     ].bitcast(I32),
                 )
 
-        def load_words(i, c, first_pass, n_passes):
+        def load_words(i, c, first_pass, n_passes, n_chunks=1):
             w = weights[i]
             if c not in w["chunks"]:
-                w["chunks"][c] = keep.tile(
-                    [P, w["passes"], N_CHUNK], I32, name="w%d_words%d" % (i, c), align_bytes=64
+                words = keep.tile(
+                    [P, w["passes"], n_chunks * N_CHUNK], I32, name="w%d_words%d" % (i, c), align_bytes=64
                 )
+                for r in range(n_chunks):
+                    w["chunks"][c + r] = words[:, :, r * N_CHUNK : (r + 1) * N_CHUNK]
+                w["tiles"][c] = words
             by_partition = w["words"].rearrange("g p n t -> p g (n t)")
             nc.sync.dma_start(
-                out=w["chunks"][c][:, first_pass : first_pass + n_passes, :],
+                out=w["tiles"][c][:, first_pass : first_pass + n_passes, :],
                 in_=by_partition[
-                    :, first_pass : first_pass + n_passes, 4 * N_CHUNK * c : 4 * N_CHUNK * (c + 1)
+                    :, first_pass : first_pass + n_passes, 4 * N_CHUNK * c : 4 * N_CHUNK * (c + n_chunks)
                 ].bitcast(I32),
             )
 
@@ -204,8 +208,8 @@ def tile_naivematryoshkalinear_kernel(
         load_words(2, 0, 6, 2)
         load_words(2, 1, 0, 4)
         load_words(2, 1, 4, 4)
-        load_words(2, 2, 0, 8)
-        load_words(2, 3, 0, 8)
+        load_words(2, 2, 0, 4, n_chunks=2)
+        load_words(2, 2, 4, 4, n_chunks=2)
 
         multiply(0, 0, 0, 1, n_tiles=2)
         multiply(0, 0, 1, 1, n_tiles=2)
@@ -226,7 +230,8 @@ def tile_naivematryoshkalinear_kernel(
         multiply(2, 0, 6, 2)
         multiply(2, 1, 0, 4)
         multiply(2, 1, 4, 4)
-        multiply(2, 2, 0, 8)
+        multiply(2, 2, 0, 4)
+        multiply(2, 2, 4, 4)
         multiply(2, 3, 0, 8, n_tiles=TOKEN_TILES - 1)
         for half in range(2):
             for g in range(weights[2]["passes"]):

@@ -190,11 +190,12 @@ def tile_naivematryoshkalinear_kernel(
         load_words(0, 0, 0, 1)
         load_words(0, 0, 1, 1)
         load_words(0, 1, 0, 2)
-        load_x_block(1)
         load_scales(weights[1], 0)
         load_words(1, 0, 0, 2)
+        load_x_block(1)
         load_words(1, 0, 2, 2)
-        load_words(1, 1, 0, 4)
+        load_words(1, 1, 0, 2)
+        load_words(1, 1, 2, 2)
         load_scales(weights[2], 0)
         load_words(2, 0, 0, 2)
         load_x_block(2)
@@ -214,12 +215,14 @@ def tile_naivematryoshkalinear_kernel(
         multiply(0, 0, 0, 1, n_tiles=2)
         multiply(0, 0, 1, 1, n_tiles=2)
         multiply(0, 0, 0, 2, first_tile=2, n_tiles=2)
-        sort_x_block(1)
         multiply(0, 1, 0, 2)
+        sort_x_block(1)
+        multiply(1, 0, 0, 2, n_tiles=2)
         quantise_x_block(1)
-        multiply(1, 0, 0, 2)
+        multiply(1, 0, 0, 2, first_tile=2, n_tiles=2)
         multiply(1, 0, 2, 2)
-        multiply(1, 1, 0, 4)
+        multiply(1, 1, 0, 2)
+        multiply(1, 1, 2, 2)
         sort_x_block(2)
         multiply(2, 0, 0, 2)
         sort_x_block(3)

from contextlib import ExitStack

import concourse.mybir as mybir
from concourse.masks import make_identity

F32 = mybir.dt.float32
BF16 = mybir.dt.bfloat16
I32 = mybir.dt.int32
U32 = mybir.dt.uint32
U8 = mybir.dt.uint8
FP8X4 = mybir.dt.float8_e4m3fn_x4

P = 128
K_PASS = 512
TOKENS = 512
TOKEN_TILES = TOKENS // P
FEATURES_IN = 4096
X_BLOCK = 1024
PASSES_PER_BLOCK = X_BLOCK // K_PASS
X_BLOCKS = FEATURES_IN // X_BLOCK
N_CHUNK = 512
PLANES_PER_TILE = 4
SCALE_ROWS = 4
QUADRANTS = 4

FLOPS = 2 * TOKENS * (1024 * 1024 + 2048 * 1024 + 4096 * 2048)


def tile_naivematryoshkalinear_kernel(
    tc, x, W0_words, W0_scales, W1_words, W1_scales, W2_words, W2_scales, out
):
    nc = tc.nc
    x_rows = x.flatten_outer_dims()
    out_rows = out.flatten_outer_dims()

    weights = [
        dict(words=W0_words, scales=W0_scales, first_column=0),
        dict(words=W1_words, scales=W1_scales, first_column=1024),
        dict(words=W2_words, scales=W2_scales, first_column=2048),
    ]
    for w in weights:
        w["passes"] = w["words"].shape[0]
        w["columns"] = w["words"].shape[2]
        w["tiles"] = {}
        w["chunks"] = {}
        w["planes"] = []

    with ExitStack() as ctx:
        ctx.enter_context(tc.manual_schedule())
        keep = ctx.enter_context(tc.tile_pool(name="keep", bufs=1))
        x_pool = ctx.enter_context(tc.tile_pool(name="x_pool", bufs=(X_BLOCKS - 1) * TOKEN_TILES))
        sorted_pool = ctx.enter_context(tc.tile_pool(name="sorted_pool", bufs=2 * TOKEN_TILES))
        stage = ctx.enter_context(tc.tile_pool(name="stage", bufs=4))
        results = ctx.enter_context(tc.tile_pool(name="results", bufs=32))
        psum_x = ctx.enter_context(tc.psum_pool(name="psum_x", bufs=4))
        psum_acc = ctx.enter_context(tc.psum_pool(name="psum_acc", bufs=4))

        identity = keep.tile([P, P], F32)
        make_identity(nc, identity[:])

        idle_operand = keep.tile([P, N_CHUNK], BF16, name="idle_operand")
        nc.vector.memset(idle_operand[:], 0.0)
        idle_bank = psum_acc.tile([P, N_CHUNK], F32, name="acc")

        def idle_matmuls(count):
            for r in range(count):
                nc.tensor.matmul(
                    out=idle_bank[:], lhsT=idle_operand[:, :P], rhs=idle_operand[:], start=True, stop=True
                )

        for i, w in enumerate(weights):
            for first_pass in range(0, w["passes"], PLANES_PER_TILE):
                planes = keep.tile(
                    [P, w["columns"]], U8, name="w%d_planes%d" % (i, first_pass), align_bytes=64
                )
                nc.vector.memset(planes[:].bitcast(I32), 0)
                w["planes"].append(planes)

        x_codes = keep.tile([P, X_BLOCKS, TOKEN_TILES, PASSES_PER_BLOCK * P], U32, align_bytes=64)
        x_scales = keep.tile([P, X_BLOCKS, TOKEN_TILES, PASSES_PER_BLOCK * P], U8, align_bytes=64)

        x_raw = {}

        def load_x_block(b):
            for m in range(TOKEN_TILES):
                raw = x_pool.tile([P, X_BLOCK], BF16, name="x_raw")
                nc.sync.dma_start(
                    out=raw[:],
                    in_=x_rows[m * P : (m + 1) * P, b * X_BLOCK : (b + 1) * X_BLOCK],
                )
                x_raw[(b, m)] = raw

        def load_scales(w, s):
            planes = w["planes"][s]
            first_pass = s * PLANES_PER_TILE
            n_passes = min(PLANES_PER_TILE, w["passes"] - first_pass)
            for q in range(QUADRANTS):
                nc.sync.dma_start(
                    out=planes[32 * q : 32 * q + SCALE_ROWS * n_passes, :].bitcast(I32),
                    in_=w["scales"][
                        first_pass : first_pass + n_passes, SCALE_ROWS * q : SCALE_ROWS * (q + 1), :
                    ].bitcast(I32),
                )

        def load_words(i, c, first_pass, n_passes, n_chunks=1):
            w = weights[i]
            if c not in w["chunks"]:
                words = keep.tile(
                    [P, w["passes"], n_chunks * N_CHUNK], I32, name="w%d_words%d" % (i, c), align_bytes=64
                )
                for r in range(n_chunks):
                    w["chunks"][c + r] = words[:, :, r * N_CHUNK : (r + 1) * N_CHUNK]
                w["tiles"][c] = words
            by_partition = w["words"].rearrange("g p n t -> p g (n t)")
            nc.sync.dma_start(
                out=w["tiles"][c][:, first_pass : first_pass + n_passes, :],
                in_=by_partition[
                    :, first_pass : first_pass + n_passes, 4 * N_CHUNK * c : 4 * N_CHUNK * (c + n_chunks)
                ].bitcast(I32),
            )


        x_sorted = {}

        def sort_x_block(b):
            for m in range(TOKEN_TILES):
                by_parity = sorted_pool.tile([P, X_BLOCK // 2], F32, name="by_parity")
                nc.vector.tensor_copy(
                    out=by_parity[:].rearrange("p (g u w) -> p g u w", g=PASSES_PER_BLOCK, u=2),
                    in_=x_raw[(b, m)][:].bitcast(F32).rearrange("p (g w u) -> p g u w", g=PASSES_PER_BLOCK, u=2),
                )
                x_sorted[(b, m)] = by_parity

        def quantise_x_block(b):
            for m in range(TOKEN_TILES):
                flipped = psum_x.tile([P, PASSES_PER_BLOCK, 2, P], F32)
                for g in range(PASSES_PER_BLOCK):
                    for u in range(2):
                        columns = x_sorted[(b, m)][:, (2 * g + u) * P : (2 * g + u + 1) * P]
                        nc.tensor.transpose(flipped[:, g, u, :], columns, identity[:])
                if b == 0:
                    idle_matmuls(1)
                grouped = stage.tile([P, PASSES_PER_BLOCK * P * 4], BF16, align_bytes=64)
                nc.scalar.copy(
                    out=grouped[:].bitcast(F32).rearrange("p (g r u) -> p g r u", g=PASSES_PER_BLOCK, u=2),
                    in_=flipped[:].rearrange("p g u r -> p g r u"),
                )
                nc.vector.quantize_mx(
                    out=x_codes[:, b, m, :].bitcast(FP8X4),
                    scales=x_scales[:, b, m, :],
                    in_=grouped[:],
                )

        open_banks = {}

        def one_pass(i, c, m, g, first=0, width=N_CHUNK):
            w = weights[i]
            if g == 0:
                acc = psum_acc.tile([P, width], F32, name="acc")
                open_banks[(i, c, m)] = acc
            acc = open_banks[(i, c, m)]
            b, g_in_block = divmod(g, PASSES_PER_BLOCK)
            tokens = slice(g_in_block * P, (g_in_block + 1) * P)
            s, j = divmod(g, PLANES_PER_TILE)
            nc.tensor.matmul_mx(
                out=acc[:],
                lhsT=x_codes[:, b, m, tokens].bitcast(FP8X4),
                lhsT_scale=x_scales[:, b, m, tokens],
                rhs=w["chunks"][c][:, g, first : first + width].bitcast(FP8X4),
                rhs_scale=w["planes"][s][SCALE_ROWS * j : P, c * N_CHUNK + first : c * N_CHUNK + first + width],
                start=(g == 0),
                stop=(g == w["passes"] - 1),
            )
            if g == w["passes"] - 1:
                result = results.tile([P, width], F32, name="result")
                if (m + first // width) % 2 == 0:
                    nc.vector.tensor_copy(out=result[:], in_=acc[:])
                else:
                    nc.scalar.copy(out=result[:], in_=acc[:])
                column = w["first_column"] + c * N_CHUNK + first
                nc.sync.dma_start(out=out_rows[m * P : (m + 1) * P, column : column + width], in_=result[:])

        def multiply(i, c, first_pass, n_passes, first_tile=0, n_tiles=TOKEN_TILES):
            for m in range(first_tile, first_tile + n_tiles):
                for g in range(first_pass, first_pass + n_passes):
                    one_pass(i, c, m, g)

        load_x_block(0)
        load_scales(weights[0], 0)
        load_words(0, 0, 0, 1)
        load_words(0, 0, 1, 1)
        load_words(0, 1, 0, 2)
        load_scales(weights[1], 0)
        load_words(1, 0, 0, 2)
        load_x_block(1)
        load_words(1, 0, 2, 2)
        load_words(1, 1, 0, 2)
        load_words(1, 1, 2, 2)
        load_scales(weights[2], 0)
        load_words(2, 0, 0, 2)
        load_x_block(2)
        load_words(2, 0, 2, 2)
        idle_matmuls(4)
        sort_x_block(0)
        quantise_x_block(0)
        load_x_block(3)
        load_scales(weights[2], 1)
        load_words(2, 0, 4, 2)
        load_words(2, 0, 6, 2)
        load_words(2, 1, 0, 4)
        load_words(2, 1, 4, 4)
        load_words(2, 2, 0, 4, n_chunks=2)
        load_words(2, 2, 4, 4, n_chunks=2)

        multiply(0, 0, 0, 1, n_tiles=2)
        multiply(0, 0, 1, 1, n_tiles=2)
        multiply(0, 0, 0, 2, first_tile=2, n_tiles=2)
        multiply(0, 1, 0, 2)
        sort_x_block(1)
        multiply(1, 0, 0, 2, n_tiles=2)
        quantise_x_block(1)
        multiply(1, 0, 0, 2, first_tile=2, n_tiles=2)
        multiply(1, 0, 2, 2)
        multiply(1, 1, 0, 2)
        multiply(1, 1, 2, 2)
        sort_x_block(2)
        multiply(2, 0, 0, 2)
        sort_x_block(3)
        quantise_x_block(2)
        multiply(2, 0, 2, 2)
        quantise_x_block(3)
        multiply(2, 0, 4, 2)
        multiply(2, 0, 6, 2)
        multiply(2, 1, 0, 4)
        multiply(2, 1, 4, 4)
        multiply(2, 2, 0, 4)
        multiply(2, 2, 4, 4)
        multiply(2, 3, 0, 8, n_tiles=TOKEN_TILES - 1)
        for half in range(2):
            for g in range(weights[2]["passes"]):
                one_pass(2, 3, TOKEN_TILES - 1, g, first=half * (N_CHUNK // 2), width=N_CHUNK // 2)
